import numpy as np
import ml_dtypes

BF16 = ml_dtypes.bfloat16


def bf(x):
    return np.asarray(x, np.float32).astype(BF16)


def f32(x):
    return np.asarray(x, np.float32)


def f64(x):
    return np.asarray(x).astype(np.float64)


def striped(idx):
    return np.tile(idx.reshape(-1, 16).T, (8, 1))


V, D, P, M, N = 2048, 128, 128, 128, 1024
MAX_NORM, TINY = 1.5, 1e-7
SELU_ALPHA, SELU_SCALE = 1.6732632423543772848170429916717, 1.0507009873554804934193349852946


def selu(v):
    return SELU_SCALE * (np.maximum(v, 0.0) + SELU_ALPHA * (np.exp(np.minimum(v, 0.0)) - 1.0))


def renorm(t):
    n = np.sqrt(np.sum(t * t, axis=1, keepdims=True))
    return t * np.minimum(1.0, MAX_NORM / np.maximum(n, TINY))


def setup_inputs():
    table = bf(np.random.uniform(0.05, 0.25, (V, 1)) * np.random.standard_normal((V, D)))
    w = bf(0.7 * np.random.standard_normal((D, M)))
    pe = bf(np.random.uniform(-0.13, 0.13, (P, N)))
    wp = bf(0.7 * np.random.standard_normal((P, M)))
    b = f32(0.2 * np.random.standard_normal((M, 1)))
    idx = np.random.permutation(np.tile(np.arange(V), 2))[:N]
    return {"table": table, "w": w, "pe": pe, "wp": wp, "b": b, "offs": striped(idx)}


def reference(table, w, pe, wp, b, offs):
    idx = offs[:16].T.reshape(-1)
    e = renorm(f64(table))
    return selu(f64(w).T @ e[idx].T + f64(wp).T @ f64(pe) + f64(b))

@@ -1,0 +1,99 @@
+import math
+
+import concourse.mybir as mybir
+from concourse.masks import make_identity
+
+BF16, F32, U16 = mybir.dt.bfloat16, mybir.dt.float32, mybir.dt.uint16
+FUNC = mybir.ActivationFunctionType
+ALU = mybir.AluOpType
+
+V, D, P, M, N = 2048, 128, 128, 128, 1024
+MAX_NORM = 1.5
+SELU_SCALE = 1.0507009873554805
+SELU_ALPHA = 1.6732632423543772
+FLOOR = SELU_SCALE * SELU_ALPHA
+
+BLOCK = 128
+BLOCKS = 4
+CHUNK = BLOCKS * BLOCK
+CHUNKS = V // CHUNK
+PIECE = 512
+PIECES = N // PIECE
+
+FLOPS = 2 * M * N * (D + P)
+
+
+def tile_dualattention_kernel(tc, table, w, pe, wp, b, offs, out):
+    nc = tc.nc
+    with (
+        tc.tile_pool(name="held", bufs=1) as held,
+        tc.tile_pool(name="chunks", bufs=CHUNKS) as chunks,
+        tc.tile_pool(name="tails", bufs=PIECES) as tails,
+        tc.psum_pool(name="flips", bufs=2) as flips,
+        tc.psum_pool(name="sums", bufs=PIECES) as sums,
+    ):
+        raws = []
+        for c in range(CHUNKS):
+            raw = chunks.tile([BLOCK, BLOCKS, D], BF16, name="raw")
+            queue = nc.sync if c % 2 == 0 else nc.scalar
+            queue.dma_start(raw[:], table[c * CHUNK : (c + 1) * CHUNK, :].rearrange("(t p) d -> p t d", p=BLOCK))
+            raws.append(raw)
+        offsets = held.tile([128, N // 16], U16, name="offsets")
+        nc.sync.dma_start(offsets[:], offs)
+        wp_sb = held.tile([P, M], BF16, name="wp_sb")
+        nc.gpsimd.dma_start(wp_sb[:], wp)
+        pe_sb = held.tile([P, N], BF16, name="pe_sb")
+        nc.gpsimd.dma_start(pe_sb[:], pe)
+        w_sb = held.tile([D, M], BF16, name="w_sb")
+        nc.gpsimd.dma_start(w_sb[:], w)
+        b_sb = held.tile([M, 1], F32, name="b_sb")
+        nc.gpsimd.dma_start(b_sb[:], b)
+
+        identity = held.tile([BLOCK, BLOCK], BF16, name="identity")
+        make_identity(nc, identity[:])
+
+        accs = []
+        for j in range(PIECES):
+            acc = sums.tile([M, PIECE], F32, name="acc")
+            nc.tensor.matmul(acc[:], wp_sb[:], pe_sb[:, j * PIECE : (j + 1) * PIECE], start=True, stop=False)
+            accs.append(acc)
+
+        clipped_t = held.tile([D, V], BF16, name="clipped_t")
+        for c in range(CHUNKS):
+            raw = raws[c]
+            norm_sq = chunks.tile([BLOCK, BLOCKS], F32, name="norm_sq")
+            for t in range(BLOCKS):
+                squares = chunks.tile([BLOCK, D], BF16, name="squares")
+                nc.scalar.activation(squares[:], raw[:, t, :], FUNC.Square, accum_out=norm_sq[:, t : t + 1])
+            over = chunks.tile([BLOCK, BLOCKS], F32, name="over")
+            nc.vector.tensor_scalar(over[:], norm_sq[:], 1.0 / (MAX_NORM * MAX_NORM), 1.0, op0=ALU.mult, op1=ALU.max)
+            root = chunks.tile([BLOCK, BLOCKS], F32, name="root")
+            nc.scalar.activation(root[:], over[:], FUNC.Sqrt)
+            shrink = chunks.tile([BLOCK, BLOCKS], F32, name="shrink")
+            nc.vector.reciprocal(shrink[:], root[:])
+            clipped = chunks.tile([BLOCK, BLOCKS, D], BF16, name="clipped")
+            flipped = flips.tile([D, CHUNK], BF16, name="flipped")
+            for t in range(BLOCKS):
+                nc.vector.tensor_scalar_mul(clipped[:, t, :], raw[:, t, :], shrink[:, t : t + 1])
+                nc.tensor.transpose(flipped[:, t * BLOCK : (t + 1) * BLOCK], clipped[:, t, :], identity[:])
+            nc.vector.tensor_copy(clipped_t[:, c * CHUNK : (c + 1) * CHUNK], flipped[:])
+
+        b_grow = held.tile([M, 1], F32, name="b_grow")
+        nc.vector.tensor_scalar_add(b_grow[:], b_sb[:], math.log(FLOOR))
+        b_pos = held.tile([M, 1], F32, name="b_pos")
+        nc.vector.tensor_scalar_mul(b_pos[:], b_sb[:], SELU_SCALE)
+
+        for j in range(PIECES):
+            picked = clipped_t[:].indirect(offsets[:, j * (PIECE // 16) : (j + 1) * (PIECE // 16)])
+            nc.tensor.matmul(accs[j][:], w_sb[:], picked, start=False, stop=True)
+
+        for j in range(PIECES):
+            grown = tails.tile([M, PIECE], F32, name="grown")
+            nc.scalar.activation(grown[:], accs[j][:], FUNC.Exp, bias=b_grow[:], scale=1.0)
+            pos = tails.tile([M, PIECE], F32, name="pos")
+            nc.scalar.activation(pos[:], accs[j][:], FUNC.Relu, bias=b_pos[:], scale=SELU_SCALE)
+            neg = tails.tile([M, PIECE], F32, name="neg")
+            nc.vector.tensor_scalar(neg[:], grown[:], FLOOR, -FLOOR, op0=ALU.min, op1=ALU.add)
+            result = tails.tile([M, PIECE], F32, name="result")
+            nc.vector.tensor_tensor(result[:], pos[:], neg[:], ALU.add)
+            nc.sync.dma_start(out[:, j * PIECE : (j + 1) * PIECE], result[:])

@@ -14,8 +14,9 @@ SELU_ALPHA = 1.6732632423543772
 FLOOR = SELU_SCALE * SELU_ALPHA
 
 BLOCK = 128
-BLOCKS = 4
-CHUNK = BLOCKS * BLOCK
+BLOCKS = V // BLOCK
+CHUNK_BLOCKS = 4
+CHUNK = CHUNK_BLOCKS * BLOCK
 CHUNKS = V // CHUNK
 PIECE = 512
 PIECES = N // PIECE
@@ -23,34 +24,39 @@ PIECES = N // PIECE
 FLOPS = 2 * M * N * (D + P)
 
 
+def column_of(t):
+    return (t % 2) * (BLOCKS // 2) + t // 2
+
+
 def tile_dualattention_kernel(tc, table, w, pe, wp, b, offs, out):
     nc = tc.nc
     with (
         tc.tile_pool(name="held", bufs=1) as held,
-        tc.tile_pool(name="chunks", bufs=CHUNKS) as chunks,
+        tc.tile_pool(name="scratch", bufs=4) as scratch,
         tc.tile_pool(name="tails", bufs=PIECES) as tails,
-        tc.psum_pool(name="flips", bufs=2) as flips,
+        tc.psum_pool(name="flips", bufs=CHUNKS) as flips,
         tc.psum_pool(name="sums", bufs=PIECES) as sums,
     ):
-        raws = []
+        identity = held.tile([BLOCK, BLOCK], BF16, name="identity")
+        make_identity(nc, identity[:])
+
+        raw = held.tile([BLOCK, BLOCKS, D], BF16, name="raw")
         for c in range(CHUNKS):
-            raw = chunks.tile([BLOCK, BLOCKS, D], BF16, name="raw")
             queue = nc.sync if c % 2 == 0 else nc.scalar
-            queue.dma_start(raw[:], table[c * CHUNK : (c + 1) * CHUNK, :].rearrange("(t p) d -> p t d", p=BLOCK))
-            raws.append(raw)
+            queue.dma_start(
+                raw[:, c * CHUNK_BLOCKS : (c + 1) * CHUNK_BLOCKS, :],
+                table[c * CHUNK : (c + 1) * CHUNK, :].rearrange("(t p) d -> p t d", p=BLOCK),
+            )
         offsets = held.tile([128, N // 16], U16, name="offsets")
         nc.sync.dma_start(offsets[:], offs)
         wp_sb = held.tile([P, M], BF16, name="wp_sb")
-        nc.gpsimd.dma_start(wp_sb[:], wp)
+        nc.sync.dma_start(wp_sb[:], wp)
         pe_sb = held.tile([P, N], BF16, name="pe_sb")
-        nc.gpsimd.dma_start(pe_sb[:], pe)
+        nc.scalar.dma_start(pe_sb[:], pe)
         w_sb = held.tile([D, M], BF16, name="w_sb")
-        nc.gpsimd.dma_start(w_sb[:], w)
+        nc.sync.dma_start(w_sb[:], w)
         b_sb = held.tile([M, 1], F32, name="b_sb")
-        nc.gpsimd.dma_start(b_sb[:], b)
-
-        identity = held.tile([BLOCK, BLOCK], BF16, name="identity")
-        make_identity(nc, identity[:])
+        nc.scalar.dma_start(b_sb[:], b)
 
         accs = []
         for j in range(PIECES):
@@ -58,25 +64,43 @@ def tile_dualattention_kernel(tc, table, w, pe, wp, b, offs, out):
             nc.tensor.matmul(acc[:], wp_sb[:], pe_sb[:, j * PIECE : (j + 1) * PIECE], start=True, stop=False)
             accs.append(acc)
 
+        norm_sq = held.tile([BLOCK, BLOCKS], F32, name="norm_sq")
+        for t in range(BLOCKS):
+            k = column_of(t)
+            if t % 2 == 0:
+                squares_v = scratch.tile([BLOCK, D], F32, name="squares_v")
+                nc.vector.scalar_tensor_tensor(
+                    squares_v[:], raw[:, t, :], 1.0, raw[:, t, :], op0=ALU.mult, op1=ALU.mult,
+                    accum_out=norm_sq[:, k : k + 1],
+                )
+            else:
+                squares_s = scratch.tile([BLOCK, D], F32, name="squares_s")
+                nc.scalar.activation(squares_s[:], raw[:, t, :], FUNC.Square, accum_out=norm_sq[:, k : k + 1])
+
+        over = held.tile([BLOCK, BLOCKS], F32, name="over")
+        nc.vector.tensor_scalar(over[:], norm_sq[:], 1.0 / (MAX_NORM * MAX_NORM), 1.0, op0=ALU.mult, op1=ALU.max)
+        root = held.tile([BLOCK, BLOCKS], F32, name="root")
+        nc.scalar.activation(root[:], over[:], FUNC.Sqrt)
+        shrink = held.tile([BLOCK, BLOCKS], F32, name="shrink")
+        nc.vector.reciprocal(shrink[:], root[:])
+
+        clipped = held.tile([BLOCK, BLOCKS, D], BF16, name="clipped")
+        flippeds = []
+        for c in range(CHUNKS):
+            flipped = flips.tile([D, CHUNK], BF16, name="flipped")
+            for s in range(CHUNK_BLOCKS):
+                t = c * CHUNK_BLOCKS + s
+                k = column_of(t)
+                nc.vector.tensor_scalar_mul(clipped[:, t, :], raw[:, t, :], shrink[:, k : k + 1])
+                nc.tensor.transpose(flipped[:, s * BLOCK : (s + 1) * BLOCK], clipped[:, t, :], identity[:])
+            flippeds.append(flipped)
+
         clipped_t = held.tile([D, V], BF16, name="clipped_t")
         for c in range(CHUNKS):
-            raw = raws[c]
-            norm_sq = chunks.tile([BLOCK, BLOCKS], F32, name="norm_sq")
-            for t in range(BLOCKS):
-                squares = chunks.tile([BLOCK, D], BF16, name="squares")
-                nc.scalar.activation(squares[:], raw[:, t, :], FUNC.Square, accum_out=norm_sq[:, t : t + 1])
-            over = chunks.tile([BLOCK, BLOCKS], F32, name="over")
-            nc.vector.tensor_scalar(over[:], norm_sq[:], 1.0 / (MAX_NORM * MAX_NORM), 1.0, op0=ALU.mult, op1=ALU.max)
-            root = chunks.tile([BLOCK, BLOCKS], F32, name="root")
-            nc.scalar.activation(root[:], over[:], FUNC.Sqrt)
-            shrink = chunks.tile([BLOCK, BLOCKS], F32, name="shrink")
-            nc.vector.reciprocal(shrink[:], root[:])
-            clipped = chunks.tile([BLOCK, BLOCKS, D], BF16, name="clipped")
-            flipped = flips.tile([D, CHUNK], BF16, name="flipped")
-            for t in range(BLOCKS):
-                nc.vector.tensor_scalar_mul(clipped[:, t, :], raw[:, t, :], shrink[:, t : t + 1])
-                nc.tensor.transpose(flipped[:, t * BLOCK : (t + 1) * BLOCK], clipped[:, t, :], identity[:])
-            nc.vector.tensor_copy(clipped_t[:, c * CHUNK : (c + 1) * CHUNK], flipped[:])
+            if c < CHUNKS // 2:
+                nc.scalar.copy(clipped_t[:, c * CHUNK : (c + 1) * CHUNK], flippeds[c][:])
+            else:
+                nc.vector.tensor_copy(clipped_t[:, c * CHUNK : (c + 1) * CHUNK], flippeds[c][:])
 
         b_grow = held.tile([M, 1], F32, name="b_grow")
         nc.vector.tensor_scalar_add(b_grow[:], b_sb[:], math.log(FLOOR))

@@ -36,6 +36,7 @@ def tile_dualattention_kernel(tc, table, w, pe, wp, b, offs, out):
         tc.tile_pool(name="tails", bufs=PIECES) as tails,
         tc.psum_pool(name="flips", bufs=CHUNKS) as flips,
         tc.psum_pool(name="sums", bufs=PIECES) as sums,
+        tc.psum_pool(name="warms", bufs=1) as warms,
     ):
         identity = held.tile([BLOCK, BLOCK], BF16, name="identity")
         make_identity(nc, identity[:])
@@ -57,6 +58,10 @@ def tile_dualattention_kernel(tc, table, w, pe, wp, b, offs, out):
         nc.sync.dma_start(w_sb[:], w)
         b_sb = held.tile([M, 1], F32, name="b_sb")
         nc.scalar.dma_start(b_sb[:], b)
+
+        warm = warms.tile([D, CHUNK], F32, name="warm")
+        for c in range(CHUNKS):
+            nc.tensor.matmul(warm[:], identity[:], raw[:, c * CHUNK_BLOCKS : (c + 1) * CHUNK_BLOCKS, :], start=True, stop=True)
 
         accs = []
         for j in range(PIECES):

@@ -59,6 +59,11 @@ def tile_dualattention_kernel(tc, table, w, pe, wp, b, offs, out):
         b_sb = held.tile([M, 1], F32, name="b_sb")
         nc.scalar.dma_start(b_sb[:], b)
 
+        one = held.tile([BLOCK, 1], F32, name="one")
+        nc.vector.memset(one[:], 1.0)
+        early_sqrt = held.tile([BLOCK, 1], F32, name="early_sqrt")
+        nc.scalar.activation(early_sqrt[:], one[:], FUNC.Sqrt)
+
         warm = warms.tile([D, CHUNK], F32, name="warm")
         for c in range(CHUNKS):
             nc.tensor.matmul(warm[:], identity[:], raw[:, c * CHUNK_BLOCKS : (c + 1) * CHUNK_BLOCKS, :], start=True, stop=True)
@@ -121,8 +126,6 @@ def tile_dualattention_kernel(tc, table, w, pe, wp, b, offs, out):
             nc.scalar.activation(grown[:], accs[j][:], FUNC.Exp, bias=b_grow[:], scale=1.0)
             pos = tails.tile([M, PIECE], F32, name="pos")
             nc.scalar.activation(pos[:], accs[j][:], FUNC.Relu, bias=b_pos[:], scale=SELU_SCALE)
-            neg = tails.tile([M, PIECE], F32, name="neg")
-            nc.vector.tensor_scalar(neg[:], grown[:], FLOOR, -FLOOR, op0=ALU.min, op1=ALU.add)
             result = tails.tile([M, PIECE], F32, name="result")
-            nc.vector.tensor_tensor(result[:], pos[:], neg[:], ALU.add)
+            nc.vector.scalar_tensor_tensor(result[:], grown[:], -FLOOR, pos[:], op0=ALU.add, op1=ALU.min)
             nc.sync.dma_start(out[:, j * PIECE : (j + 1) * PIECE], result[:])

@@ -34,8 +34,7 @@ def tile_dualattention_kernel(tc, table, w, pe, wp, b, offs, out):
         tc.tile_pool(name="held", bufs=1) as held,
         tc.tile_pool(name="scratch", bufs=4) as scratch,
         tc.tile_pool(name="tails", bufs=PIECES) as tails,
-        tc.psum_pool(name="flips", bufs=CHUNKS) as flips,
-        tc.psum_pool(name="sums", bufs=PIECES) as sums,
+        tc.psum_pool(name="banks", bufs=CHUNKS) as banks,
         tc.psum_pool(name="warms", bufs=1) as warms,
     ):
         identity = held.tile([BLOCK, BLOCK], BF16, name="identity")
@@ -68,12 +67,6 @@ def tile_dualattention_kernel(tc, table, w, pe, wp, b, offs, out):
         for c in range(CHUNKS):
             nc.tensor.matmul(warm[:], identity[:], raw[:, c * CHUNK_BLOCKS : (c + 1) * CHUNK_BLOCKS, :], start=True, stop=True)
 
-        accs = []
-        for j in range(PIECES):
-            acc = sums.tile([M, PIECE], F32, name="acc")
-            nc.tensor.matmul(acc[:], wp_sb[:], pe_sb[:, j * PIECE : (j + 1) * PIECE], start=True, stop=False)
-            accs.append(acc)
-
         norm_sq = held.tile([BLOCK, BLOCKS], F32, name="norm_sq")
         for t in range(BLOCKS):
             k = column_of(t)
@@ -97,7 +90,7 @@ def tile_dualattention_kernel(tc, table, w, pe, wp, b, offs, out):
         clipped = held.tile([BLOCK, BLOCKS, D], BF16, name="clipped")
         flippeds = []
         for c in range(CHUNKS):
-            flipped = flips.tile([D, CHUNK], BF16, name="flipped")
+            flipped = banks.tile([D, CHUNK], BF16, name="flipped", tag="bank")
             for s in range(CHUNK_BLOCKS):
                 t = c * CHUNK_BLOCKS + s
                 k = column_of(t)
@@ -111,6 +104,12 @@ def tile_dualattention_kernel(tc, table, w, pe, wp, b, offs, out):
                 nc.scalar.copy(clipped_t[:, c * CHUNK : (c + 1) * CHUNK], flippeds[c][:])
             else:
                 nc.vector.tensor_copy(clipped_t[:, c * CHUNK : (c + 1) * CHUNK], flippeds[c][:])
+
+        accs = []
+        for j in range(PIECES):
+            acc = banks.tile([M, PIECE], F32, name="acc", tag="bank")
+            nc.tensor.matmul(acc[:], wp_sb[:], pe_sb[:, j * PIECE : (j + 1) * PIECE], start=True, stop=False)
+            accs.append(acc)
 
         b_grow = held.tile([M, 1], F32, name="b_grow")
         nc.vector.tensor_scalar_add(b_grow[:], b_sb[:], math.log(FLOOR))

@@ -45,7 +45,7 @@ def tile_dualattention_kernel(tc, table, w, pe, wp, b, offs, out):
             queue = nc.sync if c % 2 == 0 else nc.scalar
             queue.dma_start(
                 raw[:, c * CHUNK_BLOCKS : (c + 1) * CHUNK_BLOCKS, :],
-                table[c * CHUNK : (c + 1) * CHUNK, :].rearrange("(t p) d -> p t d", p=BLOCK),
+                table[c * CHUNK : (c + 1) * CHUNK, :].rearrange("(p s) d -> p s d", s=CHUNK_BLOCKS),
             )
         offsets = held.tile([128, N // 16], U16, name="offsets")
         nc.sync.dma_start(offsets[:], offs)
@@ -100,10 +100,12 @@ def tile_dualattention_kernel(tc, table, w, pe, wp, b, offs, out):
 
         clipped_t = held.tile([D, V], BF16, name="clipped_t")
         for c in range(CHUNKS):
+            in_order = clipped_t[:, c * CHUNK : (c + 1) * CHUNK].rearrange("d (p s) -> d p s", s=CHUNK_BLOCKS)
+            by_block = flippeds[c][:].rearrange("d (s p) -> d p s", s=CHUNK_BLOCKS)
             if c < CHUNKS // 2:
-                nc.scalar.copy(clipped_t[:, c * CHUNK : (c + 1) * CHUNK], flippeds[c][:])
+                nc.scalar.copy(in_order, by_block)
             else:
-                nc.vector.tensor_copy(clipped_t[:, c * CHUNK : (c + 1) * CHUNK], flippeds[c][:])
+                nc.vector.tensor_copy(in_order, by_block)
 
         accs = []
         for j in range(PIECES):

@@ -60,8 +60,8 @@ def tile_dualattention_kernel(tc, table, w, pe, wp, b, offs, out):
 
         one = held.tile([BLOCK, 1], F32, name="one")
         nc.vector.memset(one[:], 1.0)
-        early_sqrt = held.tile([BLOCK, 1], F32, name="early_sqrt")
-        nc.scalar.activation(early_sqrt[:], one[:], FUNC.Sqrt)
+        early_rsqrt = held.tile([BLOCK, 1], F32, name="early_rsqrt")
+        nc.scalar.activation(early_rsqrt[:], one[:], FUNC.Abs_reciprocal_sqrt)
 
         warm = warms.tile([D, CHUNK], F32, name="warm")
         for c in range(CHUNKS):
@@ -82,10 +82,8 @@ def tile_dualattention_kernel(tc, table, w, pe, wp, b, offs, out):
 
         over = held.tile([BLOCK, BLOCKS], F32, name="over")
         nc.vector.tensor_scalar(over[:], norm_sq[:], 1.0 / (MAX_NORM * MAX_NORM), 1.0, op0=ALU.mult, op1=ALU.max)
-        root = held.tile([BLOCK, BLOCKS], F32, name="root")
-        nc.scalar.activation(root[:], over[:], FUNC.Sqrt)
         shrink = held.tile([BLOCK, BLOCKS], F32, name="shrink")
-        nc.vector.reciprocal(shrink[:], root[:])
+        nc.scalar.activation(shrink[:], over[:], FUNC.Abs_reciprocal_sqrt)
 
         clipped = held.tile([BLOCK, BLOCKS, D], BF16, name="clipped")
         flippeds = []

@@ -18,7 +18,7 @@ BLOCKS = V // BLOCK
 CHUNK_BLOCKS = 4
 CHUNK = CHUNK_BLOCKS * BLOCK
 CHUNKS = V // CHUNK
-PIECE = 512
+PIECE = 256
 PIECES = N // PIECE
 
 FLOPS = 2 * M * N * (D + P)
@@ -34,8 +34,7 @@ def tile_dualattention_kernel(tc, table, w, pe, wp, b, offs, out):
         tc.tile_pool(name="held", bufs=1) as held,
         tc.tile_pool(name="scratch", bufs=4) as scratch,
         tc.tile_pool(name="tails", bufs=PIECES) as tails,
-        tc.psum_pool(name="banks", bufs=CHUNKS) as banks,
-        tc.psum_pool(name="warms", bufs=1) as warms,
+        tc.psum_pool(name="banks", bufs=CHUNKS + 1) as banks,
     ):
         identity = held.tile([BLOCK, BLOCK], BF16, name="identity")
         make_identity(nc, identity[:])
@@ -63,7 +62,7 @@ def tile_dualattention_kernel(tc, table, w, pe, wp, b, offs, out):
         early_rsqrt = held.tile([BLOCK, 1], F32, name="early_rsqrt")
         nc.scalar.activation(early_rsqrt[:], one[:], FUNC.Abs_reciprocal_sqrt)
 
-        warm = warms.tile([D, CHUNK], F32, name="warm")
+        warm = banks.tile([D, CHUNK], F32, name="warm", tag="bank")
         for c in range(CHUNKS):
             nc.tensor.matmul(warm[:], identity[:], raw[:, c * CHUNK_BLOCKS : (c + 1) * CHUNK_BLOCKS, :], start=True, stop=True)
 

@@ -122,8 +122,15 @@ def tile_dualattention_kernel(tc, table, w, pe, wp, b, offs, out):
         for j in range(PIECES):
             grown = tails.tile([M, PIECE], F32, name="grown")
             nc.scalar.activation(grown[:], accs[j][:], FUNC.Exp, bias=b_grow[:], scale=1.0)
-            pos = tails.tile([M, PIECE], F32, name="pos")
-            nc.scalar.activation(pos[:], accs[j][:], FUNC.Relu, bias=b_pos[:], scale=SELU_SCALE)
             result = tails.tile([M, PIECE], F32, name="result")
-            nc.vector.scalar_tensor_tensor(result[:], grown[:], -FLOOR, pos[:], op0=ALU.add, op1=ALU.min)
+            if j > 0:
+                pos = tails.tile([M, PIECE], F32, name="pos")
+                nc.scalar.activation(pos[:], accs[j][:], FUNC.Relu, bias=b_pos[:], scale=SELU_SCALE)
+                nc.vector.scalar_tensor_tensor(result[:], grown[:], -FLOOR, pos[:], op0=ALU.add, op1=ALU.min)
+            else:
+                line = tails.tile([M, PIECE], F32, name="line")
+                nc.vector.tensor_scalar(line[:], accs[j][:], SELU_SCALE, b_pos[:], op0=ALU.mult, op1=ALU.add)
+                curve = tails.tile([M, PIECE], F32, name="curve")
+                nc.vector.tensor_scalar_add(curve[:], grown[:], -FLOOR)
+                nc.vector.scalar_tensor_tensor(result[:], line[:], 0.0, curve[:], op0=ALU.max, op1=ALU.min)
             nc.sync.dma_start(out[:, j * PIECE : (j + 1) * PIECE], result[:])

@@ -83,6 +83,8 @@ def tile_dualattention_kernel(tc, table, w, pe, wp, b, offs, out):
         nc.vector.tensor_scalar(over[:], norm_sq[:], 1.0 / (MAX_NORM * MAX_NORM), 1.0, op0=ALU.mult, op1=ALU.max)
         shrink = held.tile([BLOCK, BLOCKS], F32, name="shrink")
         nc.scalar.activation(shrink[:], over[:], FUNC.Abs_reciprocal_sqrt)
+        early_exp = held.tile([BLOCK, 1], F32, name="early_exp")
+        nc.scalar.activation(early_exp[:], shrink[:, 0:1], FUNC.Exp)
 
         clipped = held.tile([BLOCK, BLOCKS, D], BF16, name="clipped")
         flippeds = []
@@ -99,7 +101,7 @@ def tile_dualattention_kernel(tc, table, w, pe, wp, b, offs, out):
         for c in range(CHUNKS):
             in_order = clipped_t[:, c * CHUNK : (c + 1) * CHUNK].rearrange("d (p s) -> d p s", s=CHUNK_BLOCKS)
             by_block = flippeds[c][:].rearrange("d (s p) -> d p s", s=CHUNK_BLOCKS)
-            if c < CHUNKS // 2:
+            if c % 2 == 1:
                 nc.scalar.copy(in_order, by_block)
             else:
                 nc.vector.tensor_copy(in_order, by_block)

@@ -18,14 +18,12 @@ BLOCKS = V // BLOCK
 CHUNK_BLOCKS = 4
 CHUNK = CHUNK_BLOCKS * BLOCK
 CHUNKS = V // CHUNK
+GROUPS = 2
+GROUP_BLOCKS = BLOCKS // GROUPS
 PIECE = 256
 PIECES = N // PIECE
 
 FLOPS = 2 * M * N * (D + P)
-
-
-def column_of(t):
-    return (t % 2) * (BLOCKS // 2) + t // 2
 
 
 def tile_dualattention_kernel(tc, table, w, pe, wp, b, offs, out):
@@ -41,8 +39,7 @@ def tile_dualattention_kernel(tc, table, w, pe, wp, b, offs, out):
 
         raw = held.tile([BLOCK, BLOCKS, D], BF16, name="raw")
         for c in range(CHUNKS):
-            queue = nc.sync if c % 2 == 0 else nc.scalar
-            queue.dma_start(
+            nc.sync.dma_start(
                 raw[:, c * CHUNK_BLOCKS : (c + 1) * CHUNK_BLOCKS, :],
                 table[c * CHUNK : (c + 1) * CHUNK, :].rearrange("(p s) d -> p s d", s=CHUNK_BLOCKS),
             )
@@ -51,11 +48,11 @@ def tile_dualattention_kernel(tc, table, w, pe, wp, b, offs, out):
         wp_sb = held.tile([P, M], BF16, name="wp_sb")
         nc.sync.dma_start(wp_sb[:], wp)
         pe_sb = held.tile([P, N], BF16, name="pe_sb")
-        nc.scalar.dma_start(pe_sb[:], pe)
+        nc.sync.dma_start(pe_sb[:], pe)
         w_sb = held.tile([D, M], BF16, name="w_sb")
         nc.sync.dma_start(w_sb[:], w)
         b_sb = held.tile([M, 1], F32, name="b_sb")
-        nc.scalar.dma_start(b_sb[:], b)
+        nc.sync.dma_start(b_sb[:], b)
 
         one = held.tile([BLOCK, 1], F32, name="one")
         nc.vector.memset(one[:], 1.0)
@@ -66,25 +63,25 @@ def tile_dualattention_kernel(tc, table, w, pe, wp, b, offs, out):
         for c in range(CHUNKS):
             nc.tensor.matmul(warm[:], identity[:], raw[:, c * CHUNK_BLOCKS : (c + 1) * CHUNK_BLOCKS, :], start=True, stop=True)
 
-        norm_sq = held.tile([BLOCK, BLOCKS], F32, name="norm_sq")
-        for t in range(BLOCKS):
-            k = column_of(t)
-            if t % 2 == 0:
-                squares_v = scratch.tile([BLOCK, D], F32, name="squares_v")
-                nc.vector.scalar_tensor_tensor(
-                    squares_v[:], raw[:, t, :], 1.0, raw[:, t, :], op0=ALU.mult, op1=ALU.mult,
-                    accum_out=norm_sq[:, k : k + 1],
-                )
-            else:
-                squares_s = scratch.tile([BLOCK, D], F32, name="squares_s")
-                nc.scalar.activation(squares_s[:], raw[:, t, :], FUNC.Square, accum_out=norm_sq[:, k : k + 1])
-
-        over = held.tile([BLOCK, BLOCKS], F32, name="over")
-        nc.vector.tensor_scalar(over[:], norm_sq[:], 1.0 / (MAX_NORM * MAX_NORM), 1.0, op0=ALU.mult, op1=ALU.max)
-        shrink = held.tile([BLOCK, BLOCKS], F32, name="shrink")
-        nc.scalar.activation(shrink[:], over[:], FUNC.Abs_reciprocal_sqrt)
-        early_exp = held.tile([BLOCK, 1], F32, name="early_exp")
-        nc.scalar.activation(early_exp[:], shrink[:, 0:1], FUNC.Exp)
+        shrinks = []
+        for g in range(GROUPS):
+            norm_sq = held.tile([BLOCK, GROUP_BLOCKS], F32, name=f"norm_sq{g}")
+            for i in range(GROUP_BLOCKS):
+                t = g * GROUP_BLOCKS + i
+                if i % 2 == 0:
+                    squares_v = scratch.tile([BLOCK, D], F32, name="squares_v")
+                    nc.vector.scalar_tensor_tensor(
+                        squares_v[:], raw[:, t, :], 1.0, raw[:, t, :], op0=ALU.mult, op1=ALU.mult,
+                        accum_out=norm_sq[:, i : i + 1],
+                    )
+                else:
+                    squares_s = scratch.tile([BLOCK, D], F32, name="squares_s")
+                    nc.scalar.activation(squares_s[:], raw[:, t, :], FUNC.Square, accum_out=norm_sq[:, i : i + 1])
+            over = held.tile([BLOCK, GROUP_BLOCKS], F32, name=f"over{g}")
+            nc.vector.tensor_scalar(over[:], norm_sq[:], 1.0 / (MAX_NORM * MAX_NORM), 1.0, op0=ALU.mult, op1=ALU.max)
+            shrink = held.tile([BLOCK, GROUP_BLOCKS], F32, name=f"shrink{g}")
+            nc.scalar.activation(shrink[:], over[:], FUNC.Abs_reciprocal_sqrt)
+            shrinks.append(shrink)
 
         clipped = held.tile([BLOCK, BLOCKS, D], BF16, name="clipped")
         flippeds = []
@@ -92,8 +89,8 @@ def tile_dualattention_kernel(tc, table, w, pe, wp, b, offs, out):
             flipped = banks.tile([D, CHUNK], BF16, name="flipped", tag="bank")
             for s in range(CHUNK_BLOCKS):
                 t = c * CHUNK_BLOCKS + s
-                k = column_of(t)
-                nc.vector.tensor_scalar_mul(clipped[:, t, :], raw[:, t, :], shrink[:, k : k + 1])
+                g, i = divmod(t, GROUP_BLOCKS)
+                nc.vector.tensor_scalar_mul(clipped[:, t, :], raw[:, t, :], shrinks[g][:, i : i + 1])
                 nc.tensor.transpose(flipped[:, s * BLOCK : (s + 1) * BLOCK], clipped[:, t, :], identity[:])
             flippeds.append(flipped)
 
@@ -101,7 +98,7 @@ def tile_dualattention_kernel(tc, table, w, pe, wp, b, offs, out):
         for c in range(CHUNKS):
             in_order = clipped_t[:, c * CHUNK : (c + 1) * CHUNK].rearrange("d (p s) -> d p s", s=CHUNK_BLOCKS)
             by_block = flippeds[c][:].rearrange("d (s p) -> d p s", s=CHUNK_BLOCKS)
-            if c % 2 == 1:
+            if c == 1:
                 nc.scalar.copy(in_order, by_block)
             else:
                 nc.vector.tensor_copy(in_order, by_block)

@@ -91,7 +91,7 @@ def tile_dualattention_kernel(tc, table, w, pe, wp, b, offs, out):
                 t = c * CHUNK_BLOCKS + s
                 g, i = divmod(t, GROUP_BLOCKS)
                 nc.vector.tensor_scalar_mul(clipped[:, t, :], raw[:, t, :], shrinks[g][:, i : i + 1])
-                nc.tensor.transpose(flipped[:, s * BLOCK : (s + 1) * BLOCK], clipped[:, t, :], identity[:])
+                nc.tensor.matmul(flipped[:, s * BLOCK : (s + 1) * BLOCK], clipped[:, t, :], identity[:], start=True, stop=True)
             flippeds.append(flipped)
 
         clipped_t = held.tile([D, V], BF16, name="clipped_t")

@@ -125,7 +125,9 @@ def tile_dualattention_kernel(tc, table, w, pe, wp, b, offs, out):
             if j > 0:
                 pos = tails.tile([M, PIECE], F32, name="pos")
                 nc.scalar.activation(pos[:], accs[j][:], FUNC.Relu, bias=b_pos[:], scale=SELU_SCALE)
-                nc.vector.scalar_tensor_tensor(result[:], grown[:], -FLOOR, pos[:], op0=ALU.add, op1=ALU.min)
+                curve = tails.tile([M, PIECE], F32, name="curve")
+                nc.vector.tensor_scalar_add(curve[:], grown[:], -FLOOR)
+                nc.vector.tensor_tensor(result[:], curve[:], pos[:], ALU.min)
             else:
                 line = tails.tile([M, PIECE], F32, name="line")
                 nc.vector.tensor_scalar(line[:], accs[j][:], SELU_SCALE, b_pos[:], op0=ALU.mult, op1=ALU.add)

import math

import concourse.mybir as mybir
from concourse.masks import make_identity

BF16, F32, U16 = mybir.dt.bfloat16, mybir.dt.float32, mybir.dt.uint16
FUNC = mybir.ActivationFunctionType
ALU = mybir.AluOpType

V, D, P, M, N = 2048, 128, 128, 128, 1024
MAX_NORM = 1.5
SELU_SCALE = 1.0507009873554805
SELU_ALPHA = 1.6732632423543772
FLOOR = SELU_SCALE * SELU_ALPHA

BLOCK = 128
BLOCKS = V // BLOCK
CHUNK_BLOCKS = 4
CHUNK = CHUNK_BLOCKS * BLOCK
CHUNKS = V // CHUNK
GROUPS = 2
GROUP_BLOCKS = BLOCKS // GROUPS
PIECE = 256
PIECES = N // PIECE

FLOPS = 2 * M * N * (D + P)


def tile_dualattention_kernel(tc, table, w, pe, wp, b, offs, out):
    nc = tc.nc
    with (
        tc.tile_pool(name="held", bufs=1) as held,
        tc.tile_pool(name="scratch", bufs=4) as scratch,
        tc.tile_pool(name="tails", bufs=PIECES) as tails,
        tc.psum_pool(name="banks", bufs=CHUNKS + 1) as banks,
    ):
        identity = held.tile([BLOCK, BLOCK], BF16, name="identity")
        make_identity(nc, identity[:])

        raw = held.tile([BLOCK, BLOCKS, D], BF16, name="raw")
        for c in range(CHUNKS):
            nc.sync.dma_start(
                raw[:, c * CHUNK_BLOCKS : (c + 1) * CHUNK_BLOCKS, :],
                table[c * CHUNK : (c + 1) * CHUNK, :].rearrange("(p s) d -> p s d", s=CHUNK_BLOCKS),
            )
        offsets = held.tile([128, N // 16], U16, name="offsets")
        nc.sync.dma_start(offsets[:], offs)
        wp_sb = held.tile([P, M], BF16, name="wp_sb")
        nc.sync.dma_start(wp_sb[:], wp)
        pe_sb = held.tile([P, N], BF16, name="pe_sb")
        nc.sync.dma_start(pe_sb[:], pe)
        w_sb = held.tile([D, M], BF16, name="w_sb")
        nc.sync.dma_start(w_sb[:], w)
        b_sb = held.tile([M, 1], F32, name="b_sb")
        nc.sync.dma_start(b_sb[:], b)

        one = held.tile([BLOCK, 1], F32, name="one")
        nc.vector.memset(one[:], 1.0)
        early_rsqrt = held.tile([BLOCK, 1], F32, name="early_rsqrt")
        nc.scalar.activation(early_rsqrt[:], one[:], FUNC.Abs_reciprocal_sqrt)

        warm = banks.tile([D, CHUNK], F32, name="warm", tag="bank")
        for c in range(CHUNKS):
            nc.tensor.matmul(warm[:], identity[:], raw[:, c * CHUNK_BLOCKS : (c + 1) * CHUNK_BLOCKS, :], start=True, stop=True)

        shrinks = []
        for g in range(GROUPS):
            norm_sq = held.tile([BLOCK, GROUP_BLOCKS], F32, name=f"norm_sq{g}")
            for i in range(GROUP_BLOCKS):
                t = g * GROUP_BLOCKS + i
                if i % 2 == 0:
                    squares_v = scratch.tile([BLOCK, D], F32, name="squares_v")
                    nc.vector.scalar_tensor_tensor(
                        squares_v[:], raw[:, t, :], 1.0, raw[:, t, :], op0=ALU.mult, op1=ALU.mult,
                        accum_out=norm_sq[:, i : i + 1],
                    )
                else:
                    squares_s = scratch.tile([BLOCK, D], F32, name="squares_s")
                    nc.scalar.activation(squares_s[:], raw[:, t, :], FUNC.Square, accum_out=norm_sq[:, i : i + 1])
            over = held.tile([BLOCK, GROUP_BLOCKS], F32, name=f"over{g}")
            nc.vector.tensor_scalar(over[:], norm_sq[:], 1.0 / (MAX_NORM * MAX_NORM), 1.0, op0=ALU.mult, op1=ALU.max)
            shrink = held.tile([BLOCK, GROUP_BLOCKS], F32, name=f"shrink{g}")
            nc.scalar.activation(shrink[:], over[:], FUNC.Abs_reciprocal_sqrt)
            shrinks.append(shrink)

        clipped = held.tile([BLOCK, BLOCKS, D], BF16, name="clipped")
        flippeds = []
        for c in range(CHUNKS):
            flipped = banks.tile([D, CHUNK], BF16, name="flipped", tag="bank")
            for s in range(CHUNK_BLOCKS):
                t = c * CHUNK_BLOCKS + s
                g, i = divmod(t, GROUP_BLOCKS)
                nc.vector.tensor_scalar_mul(clipped[:, t, :], raw[:, t, :], shrinks[g][:, i : i + 1])
                nc.tensor.matmul(flipped[:, s * BLOCK : (s + 1) * BLOCK], clipped[:, t, :], identity[:], start=True, stop=True)
            flippeds.append(flipped)

        clipped_t = held.tile([D, V], BF16, name="clipped_t")
        for c in range(CHUNKS):
            in_order = clipped_t[:, c * CHUNK : (c + 1) * CHUNK].rearrange("d (p s) -> d p s", s=CHUNK_BLOCKS)
            by_block = flippeds[c][:].rearrange("d (s p) -> d p s", s=CHUNK_BLOCKS)
            if c == 1:
                nc.scalar.copy(in_order, by_block)
            else:
                nc.vector.tensor_copy(in_order, by_block)

        accs = []
        for j in range(PIECES):
            acc = banks.tile([M, PIECE], F32, name="acc", tag="bank")
            nc.tensor.matmul(acc[:], wp_sb[:], pe_sb[:, j * PIECE : (j + 1) * PIECE], start=True, stop=False)
            accs.append(acc)

        b_grow = held.tile([M, 1], F32, name="b_grow")
        nc.vector.tensor_scalar_add(b_grow[:], b_sb[:], math.log(FLOOR))
        b_pos = held.tile([M, 1], F32, name="b_pos")
        nc.vector.tensor_scalar_mul(b_pos[:], b_sb[:], SELU_SCALE)

        for j in range(PIECES):
            picked = clipped_t[:].indirect(offsets[:, j * (PIECE // 16) : (j + 1) * (PIECE // 16)])
            nc.tensor.matmul(accs[j][:], w_sb[:], picked, start=False, stop=True)

        for j in range(PIECES):
            grown = tails.tile([M, PIECE], F32, name="grown")
            nc.scalar.activation(grown[:], accs[j][:], FUNC.Exp, bias=b_grow[:], scale=1.0)
            result = tails.tile([M, PIECE], F32, name="result")
            if j > 0:
                pos = tails.tile([M, PIECE], F32, name="pos")
                nc.scalar.activation(pos[:], accs[j][:], FUNC.Relu, bias=b_pos[:], scale=SELU_SCALE)
                curve = tails.tile([M, PIECE], F32, name="curve")
                nc.vector.tensor_scalar_add(curve[:], grown[:], -FLOOR)
                nc.vector.tensor_tensor(result[:], curve[:], pos[:], ALU.min)
            else:
                line = tails.tile([M, PIECE], F32, name="line")
                nc.vector.tensor_scalar(line[:], accs[j][:], SELU_SCALE, b_pos[:], op0=ALU.mult, op1=ALU.add)
                curve = tails.tile([M, PIECE], F32, name="curve")
                nc.vector.tensor_scalar_add(curve[:], grown[:], -FLOOR)
                nc.vector.scalar_tensor_tensor(result[:], line[:], 0.0, curve[:], op0=ALU.max, op1=ALU.min)
            nc.sync.dma_start(out[:, j * PIECE : (j + 1) * PIECE], result[:])
